import numpy as np
import ml_dtypes


def mxq(x, axis, fmt="e4m3"):
    dtype, down = {"e4m3": (ml_dtypes.float8_e4m3fn, 7), "e5m2": (ml_dtypes.float8_e5m2, 14)}[fmt]
    v = np.moveaxis(np.asarray(x, np.float32).astype(ml_dtypes.bfloat16).astype(np.float64), axis, -1)
    blocks = v.reshape(v.shape[:-1] + (-1, 32))
    amax = np.abs(blocks).max(-1, keepdims=True)
    byte = np.maximum(np.where(amax > 0, np.frexp(amax)[1] - 1 + 127, 0) - down, 1)
    scale = np.exp2(byte - 127.0)
    codes = (blocks / scale).astype(np.float32).astype(dtype).astype(np.float64)
    return np.moveaxis((codes * scale).reshape(v.shape), -1, axis)


WIDE = False


def mx_kscale(k):
    if not WIDE:
        return np.ones(k)
    levels = np.array([10, -10, 5, -5, 0])
    if k % 512:
        return np.exp2(np.random.permutation(np.resize(levels, k // 32))).repeat(32)
    a = np.empty((k // 512, 16))
    for p in range(k // 512):
        a[p, :8] = np.random.permutation(np.resize(levels, 8))
        for g in range(8):
            far = levels[np.abs(levels - a[p, g]) >= 10]
            a[p, g + 8] = far[np.random.randint(len(far))]
    return np.exp2(a.ravel()).repeat(32)


BF16 = ml_dtypes.bfloat16


def bf(x):
    return np.asarray(x, np.float32).astype(BF16)


def f64(x):
    return np.asarray(x).astype(np.float64)


M, N, E, P, S, B, KT = 1024, 512, 16, 32, 17, 128, 2


def setup_inputs():
    s = mx_kscale(M)
    return {
        "z": bf(np.random.standard_normal((M, B)) * s[:, None]),
        "mlp_out": bf(np.random.standard_normal((B, E)) * 0.65),
        "t2": bf(0.5 + 0.1 * np.random.random_sample(1)),
        "A": bf(np.random.standard_normal((E, M)) * 0.5 / s),
        "W": bf(np.random.standard_normal((E, M, M)) / np.sqrt(M) / s),
        "h": bf(np.random.standard_normal((E, M)) * 0.1),
    }


def reference(z, mlp_out, t2, A, W, h):
    z = f64(z)
    lg = -f64(mlp_out).T / f64(t2)[0]
    ex = np.exp(lg - lg.max(axis=0, keepdims=True))
    w_exp = ex / ex.sum(axis=0, keepdims=True)
    zcat = np.concatenate([z[:-P], np.maximum(z[-P:], 0.0)], axis=0)
    Az = f64(A)[:, :, None] * z[None, :, :]
    Wz = mxq(f64(W), 2, "e4m3") @ mxq(zcat, 0, "e4m3")
    expert_out = Az + Wz + f64(h)[:, :, None]
    return np.sum(expert_out * w_exp[:, None, :], axis=0)

@@ -1,0 +1,304 @@
+from contextlib import ExitStack
+
+import concourse.mybir as mybir
+from concourse.masks import make_identity
+
+F32 = mybir.dt.float32
+BF16 = mybir.dt.bfloat16
+I32 = mybir.dt.int32
+U32 = mybir.dt.uint32
+U8 = mybir.dt.uint8
+FP8X4 = mybir.dt.float8_e4m3fn_x4
+ALU = mybir.AluOpType
+ACT = mybir.ActivationFunctionType
+AX = mybir.AxisListType
+
+P = 128
+M = 1024
+E = 16
+B = 128
+FLOPS = 2 * E * M * M * B + 4 * E * M * B
+
+PIN = True
+W_BUFS = 12
+TP_BUFS = 5
+LAG_M = 3
+LAG_S = 4
+PRE_WARM = 7
+WARM_UNITS = 3
+WARM_BANKS = (0, 1, 3)
+V_LAST = 28
+V_PERIOD = 4
+
+
+def make_units():
+    units = []
+    for e in range(E - 2):
+        units.append((e, 0, 4))
+        units.append((e, 4, 4))
+    units.extend([(E - 2, 0, 4), (E - 1, 0, 4), (E - 2, 4, 4), (E - 1, 4, 2), (E - 1, 6, 2)])
+    return units
+
+
+def tile_dynamix_pb_kernel(tc, z, mlp_out, t2, A, W, h, out):
+    nc = tc.nc
+    units = make_units()
+    nu = len(units)
+    finish_after = {29: (0, 4), 31: (4, 2), 32: (6, 2)}
+    with ExitStack() as ctx:
+        const = ctx.enter_context(tc.tile_pool(name="const", bufs=1))
+        wpool = ctx.enter_context(tc.tile_pool(name="wpool", bufs=W_BUFS))
+        gpool = ctx.enter_context(tc.tile_pool(name="gpool", bufs=3))
+        qpool = ctx.enter_context(tc.tile_pool(name="qpool", bufs=4))
+        opool = ctx.enter_context(tc.tile_pool(name="opool", bufs=2))
+        pt = ctx.enter_context(tc.psum_pool(name="pt", bufs=TP_BUFS))
+        pm = ctx.enter_context(tc.psum_pool(name="pm", bufs=8 - TP_BUFS))
+        if PIN:
+            ctx.enter_context(tc.manual_schedule())
+
+        w_tiles = {}
+
+        def load_w(i, pieces=1):
+            e, t0, nt = units[i]
+            wt = wpool.tile([P, 4 * M], BF16, name="wt", tag="wt")
+            src = W[e].rearrange("(p t) k -> p (t k)", t=8)
+            step = nt * M // pieces
+            for c in range(pieces):
+                nc.sync.dma_start(
+                    out=wt[:, c * step:(c + 1) * step], in_=src[:, t0 * M + c * step:t0 * M + (c + 1) * step]
+                )
+            w_tiles[i] = wt
+
+        warm = const.tile([P, 1], F32, name="warm")
+        nc.vector.memset(warm[:], 0.0)
+        dz = const.tile([P, 512], BF16, name="dz")
+        nc.vector.memset(dz[:].bitcast(I32), 0)
+        ah = const.tile([P, 2 * M], BF16, name="ah")
+        nc.vector.memset(ah[:].bitcast(I32), 0)
+        xs = const.tile([P, P], BF16, name="xs")
+        nc.vector.memset(xs[:].bitcast(I32), 0)
+        warm2 = const.tile([P, 1], F32, name="warm2")
+        nc.scalar.activation(out=warm2[:], in_=warm[:], func=ACT.Exp)
+
+        mlp = const.tile([P, E], BF16, name="mlp")
+        nc.sync.dma_start(out=mlp[:], in_=mlp_out)
+        t2b = const.tile([P, 1], BF16, name="t2b")
+        nc.sync.dma_start(out=t2b[:], in_=t2.partition_broadcast(P))
+        load_w(0, pieces=2)
+        zq = const.tile([P, 8 * B], BF16, name="zq")
+        nc.sync.dma_start(
+            out=zq[:].rearrange("p (c x) -> p c x", c=2),
+            in_=z.rearrange("(c p e) b -> p c (e b)", c=2, p=P, e=4),
+        )
+        for i in range(1, 4):
+            load_w(i)
+        for s in range(3):
+            nc.sync.dma_start(out=ah[16 * s:16 * s + 16, 0:M], in_=A)
+            nc.sync.dma_start(out=ah[16 * s:16 * s + 16, M:2 * M], in_=h)
+        zm = const.tile([P, 8 * B], BF16, name="zm")
+        nc.sync.dma_start(out=zm[:], in_=z.rearrange("(p t) b -> p (t b)", t=8))
+        for i in range(4, W_BUFS):
+            load_w(i)
+
+        dps = pm.tile([P, 512], F32, name="dps", tag="ps")
+
+        def dummy():
+            nc.tensor.matmul(dps[:], lhsT=dz[:, 0:P], rhs=dz[:], start=True, stop=True)
+
+        for c in range(PRE_WARM):
+            dummy()
+
+        ident_f = const.tile([P, P], F32, name="ident_f")
+        make_identity(nc, ident_f[:])
+        ident_b = const.tile([P, P], BF16, name="ident_b")
+        make_identity(nc, ident_b[:])
+        aht = const.tile([P, 2 * M], BF16, name="aht")
+        nc.gpsimd.tensor_scalar(
+            out=aht[:].rearrange("k (a t p) -> k a t p", a=2, t=8),
+            in0=ah[:].rearrange("k (a p t) -> k a t p", a=2, t=8),
+            scalar1=1.0, scalar2=0.0, op0=ALU.mult, op1=ALU.add,
+        )
+
+        mask = const.tile([P, 1], F32, name="mask")
+        nc.vector.tensor_reduce(out=mask[:], in_=ident_f[:, 120:128], axis=AX.X, op=ALU.add)
+        floor = const.tile([P, 1], F32, name="floor")
+        nc.vector.tensor_scalar(out=floor[:], in0=mask[:], scalar1=-1.0, scalar2=3.4e38, op0=ALU.add, op1=ALU.mult)
+
+        rt = const.tile([P, 1], F32, name="rt")
+        nc.vector.reciprocal(out=rt[:], in_=t2b[:])
+        lg = const.tile([P, E], F32, name="lg")
+        nc.vector.tensor_scalar(out=lg[:], in0=mlp[:], scalar1=rt[:, 0:1], scalar2=-1.0, op0=ALU.mult, op1=ALU.mult)
+        mx = const.tile([P, 1], F32, name="mx")
+        nc.vector.tensor_reduce(out=mx[:], in_=lg[:], axis=AX.X, op=ALU.max)
+        nmx = const.tile([P, 1], F32, name="nmx")
+        nc.vector.tensor_scalar(out=nmx[:], in0=mx[:], scalar1=-1.0, scalar2=None, op0=ALU.mult)
+        ex = const.tile([P, E], F32, name="ex")
+        sm = const.tile([P, 1], F32, name="sm")
+        rs = const.tile([P, 1], F32, name="rs")
+        wg = const.tile([P, E], F32, name="wg")
+        zg = const.tile([P, 8 * B], BF16, name="zg", align_bytes=64)
+        zc = const.tile([P, 2 * B], U32, name="zc", align_bytes=64)
+        zs = const.tile([P, 2 * B], U8, name="zs", align_bytes=64)
+        acc = const.tile([P, M], F32, name="acc")
+        rw = const.tile([P, B], BF16, name="rw")
+        zt = const.tile([P, M], BF16, name="zt")
+
+        def gate_exp():
+            nc.scalar.activation(out=ex[:], in_=lg[:], func=ACT.Exp, bias=nmx[:, 0:1], scale=1.0, accum_out=sm[:])
+
+        def z_and_gate():
+            nc.vector.tensor_scalar(
+                out=zq[:, 512:1024], in0=zq[:, 512:1024], scalar1=floor[:, 0:1], scalar2=None, op0=ALU.max
+            )
+            nc.vector.tensor_copy(
+                out=zg[:].rearrange("p (g b j) -> p g b j", g=2, j=4),
+                in_=zq[:].rearrange("p (g j b) -> p g b j", g=2, j=4),
+            )
+            nc.vector.reciprocal(out=rs[:], in_=sm[:])
+            nc.vector.tensor_scalar(out=wg[:], in0=ex[:], scalar1=rs[:, 0:1], scalar2=None, op0=ALU.mult)
+            nc.vector.quantize_mx(out=zc[:].bitcast(FP8X4), scales=zs[:], in_=zg[:])
+
+        def gate_split():
+            nc.vector.tensor_copy(out=xs[:, 0:16], in_=wg[:])
+            r1 = const.tile([P, E], F32, name="r1")
+            nc.vector.tensor_tensor(out=r1[:], in0=wg[:], in1=xs[:, 0:16], op=ALU.subtract)
+            nc.vector.tensor_copy(out=xs[:, 16:32], in_=r1[:])
+            r2 = const.tile([P, E], F32, name="r2")
+            nc.vector.tensor_tensor(out=r2[:], in0=r1[:], in1=xs[:, 16:32], op=ALU.subtract)
+            nc.vector.tensor_copy(out=xs[:, 32:48], in_=r2[:])
+
+        side = {}
+
+        def side_tensor(s):
+            if s == 4:
+                xp = pt.tile([P, P], BF16, name="xp", tag="tp")
+                nc.tensor.transpose(xp[:], xs[:], ident_b[:])
+                side["xp"] = xp
+                zp = pt.tile([P, M], BF16, name="zp", tag="tp")
+                for t in range(8):
+                    nc.tensor.transpose(zp[:, t * P:(t + 1) * P], zm[:, t * P:(t + 1) * P], ident_b[:])
+                nc.scalar.copy(out=zt[:], in_=zp[:])
+            if 6 <= s <= 9:
+                hb, a = divmod(s - 6, 2)
+                gb = pt.tile([P, 512], F32, name="gb", tag="tp")
+                col = (a * 8 + 4 * hb) * P
+                nc.tensor.matmul(gb[:], lhsT=rw[:], rhs=aht[:, col:col + 512], start=True, stop=True)
+                side["gb"] = gb
+
+        def side_vector(s):
+            if s == 2:
+                gate_split()
+            if s == 4:
+                nc.vector.tensor_copy(out=rw[:], in_=side["xp"][:])
+            if 6 <= s <= 9:
+                hb, a = divmod(s - 6, 2)
+                sl = slice(hb * 512, (hb + 1) * 512)
+                if a == 0:
+                    tmp = opool.tile([P, 512], F32, name="tmp", tag="tmp")
+                    nc.vector.tensor_tensor(out=tmp[:], in0=side["gb"][:], in1=zt[:, sl], op=ALU.mult)
+                    side["tmp"] = tmp
+                else:
+                    nc.vector.tensor_tensor(out=side["tmp"][:], in0=side["gb"][:], in1=side["tmp"][:], op=ALU.add)
+                    nc.vector.tensor_tensor(out=acc[:, sl], in0=acc[:, sl], in1=side["tmp"][:], op=ALU.add)
+
+        g_tiles = {}
+        q_tiles = {}
+        m_tiles = {}
+
+        def transposes(i):
+            e, t0, nt = units[i]
+            w32 = w_tiles[i][:].bitcast(F32)
+            gt = gpool.tile([P, 4096], BF16, name="gt", tag="gt", align_bytes=64)
+            g32 = gt[:].bitcast(F32)
+            for tp in range(nt // 2):
+                for g in range(2):
+                    bank = pt.tile([P, 512], F32, name="bank", tag="tp")
+                    for u in range(2):
+                        for t_ in range(2):
+                            col = (2 * tp + t_) * 512 + 256 * g
+                            pos = (2 * u + t_) * P
+                            nc.tensor.transpose(bank[:, pos:pos + P], w32[:, col + u:col + 256:2], ident_f[:])
+                    off = g * nt * 256 + tp * 512
+                    dst = g32[:, off:off + 512].rearrange("p (c u) -> p c u", u=2)
+                    srcv = bank[:].rearrange("p (u c) -> p c u", u=2)
+                    if i % V_PERIOD == 0 and 0 < i < V_LAST and tp == 1 and g == 1:
+                        nc.vector.tensor_copy(out=dst, in_=srcv)
+                    else:
+                        nc.scalar.copy(out=dst, in_=srcv)
+                    if i < WARM_UNITS and 2 * tp + g in WARM_BANKS:
+                        dummy()
+                if i == 0 and tp == 0:
+                    gate_exp()
+            g_tiles[i] = gt
+
+        def quantise(i):
+            nt = units[i][2]
+            cw = qpool.tile([P, 1024], U32, name="cw", tag="cw", align_bytes=64)
+            cs = qpool.tile([P, 1024], U8, name="cs", tag="cs", align_bytes=64)
+            nc.vector.quantize_mx(
+                out=cw[:, 0:nt * 256].bitcast(FP8X4), scales=cs[:, 0:nt * 256], in_=g_tiles[i][:, 0:nt * 1024]
+            )
+            q_tiles[i] = (cw, cs)
+
+        def multiply(i):
+            e, t0, nt = units[i]
+            cw, cs = q_tiles[i]
+            n = nt * P
+            ps = pm.tile([P, 512], F32, name="ps", tag="ps")
+            c0 = 0
+            for g in range(2):
+                nc.tensor.matmul_mx(
+                    out=ps[:, c0:c0 + n],
+                    lhsT=zc[:, g * B:(g + 1) * B].bitcast(FP8X4),
+                    lhsT_scale=zs[:, g * B:(g + 1) * B],
+                    rhs=cw[:, g * n:(g + 1) * n].bitcast(FP8X4),
+                    rhs_scale=cs[:, g * n:(g + 1) * n],
+                    start=(g == 0),
+                    stop=(g == 1),
+                )
+            m_tiles[i] = (ps, c0)
+
+        def mix(i):
+            e, t0, nt = units[i]
+            ps, c0 = m_tiles[i]
+            sl = slice(t0 * P, (t0 + nt) * P)
+            if e == 0:
+                nc.vector.tensor_scalar(
+                    out=acc[:, sl], in0=ps[:, c0:c0 + nt * P], scalar1=wg[:, 0:1], scalar2=None, op0=ALU.mult
+                )
+            else:
+                nc.vector.scalar_tensor_tensor(
+                    out=acc[:, sl], in0=ps[:, c0:c0 + nt * P], scalar=wg[:, e:e + 1], in1=acc[:, sl],
+                    op0=ALU.mult, op1=ALU.add,
+                )
+
+        def finish(t0, nt):
+            fb = pt.tile([P, 512], F32, name="fb", tag="tp")
+            for tl in range(nt):
+                col = (t0 + tl) * P
+                nc.tensor.transpose(fb[:, tl * P:(tl + 1) * P], acc[:, col:col + P], ident_f[:])
+            fin = opool.tile([P, 512], F32, name="fin", tag="fin")
+            nc.scalar.copy(out=fin[:, 0:nt * P], in_=fb[:, 0:nt * P])
+            nc.sync.dma_start(
+                out=out.rearrange("(p t) b -> p (t b)", t=8)[:, t0 * P:(t0 + nt) * P], in_=fin[:, 0:nt * P]
+            )
+
+        next_load = W_BUFS
+        for s in range(nu + max(LAG_M, LAG_S)):
+            if s < nu:
+                transposes(s)
+                if next_load < nu:
+                    load_w(next_load)
+                    next_load += 1
+            side_tensor(s)
+            if s == 0:
+                z_and_gate()
+            if 0 <= s - LAG_M < nu:
+                multiply(s - LAG_M)
+            if 0 <= s - LAG_S < nu:
+                mix(s - LAG_S)
+                if s - LAG_S in finish_after:
+                    finish(finish_after[s - LAG_S][0], finish_after[s - LAG_S][1])
+            if 1 <= s <= nu:
+                quantise(s - 1)
+            side_vector(s)

@@ -27,8 +27,7 @@ LAG_S = 4
 PRE_WARM = 7
 WARM_UNITS = 3
 WARM_BANKS = (0, 1, 3)
-V_LAST = 28
-V_PERIOD = 4
+FIRST_SORTED = 2
 
 
 def make_units():
@@ -51,6 +50,7 @@ def tile_dynamix_pb_kernel(tc, z, mlp_out, t2, A, W, h, out):
         gpool = ctx.enter_context(tc.tile_pool(name="gpool", bufs=3))
         qpool = ctx.enter_context(tc.tile_pool(name="qpool", bufs=4))
         opool = ctx.enter_context(tc.tile_pool(name="opool", bufs=2))
+        spool = ctx.enter_context(tc.tile_pool(name="spool", bufs=3))
         pt = ctx.enter_context(tc.psum_pool(name="pt", bufs=TP_BUFS))
         pm = ctx.enter_context(tc.psum_pool(name="pm", bufs=8 - TP_BUFS))
         if PIN:
@@ -205,6 +205,19 @@ def tile_dynamix_pb_kernel(tc, z, mlp_out, t2, A, W, h, out):
         q_tiles = {}
         m_tiles = {}
 
+        s_tiles = {}
+
+        def sorts(i):
+            return FIRST_SORTED <= i < nu and units[i][2] == 4
+
+        def sort_words(i):
+            st = spool.tile([P, 1024], F32, name="st", tag="st")
+            nc.vector.tensor_copy(
+                out=st[:].rearrange("p (x u k) -> p x u k", x=4, u=2),
+                in_=w_tiles[i][:, 0:2048].bitcast(F32).rearrange("p (x k u) -> p x u k", x=4, u=2),
+            )
+            s_tiles[i] = st
+
         def transposes(i):
             e, t0, nt = units[i]
             w32 = w_tiles[i][:].bitcast(F32)
@@ -217,14 +230,15 @@ def tile_dynamix_pb_kernel(tc, z, mlp_out, t2, A, W, h, out):
                         for t_ in range(2):
                             col = (2 * tp + t_) * 512 + 256 * g
                             pos = (2 * u + t_) * P
-                            nc.tensor.transpose(bank[:, pos:pos + P], w32[:, col + u:col + 256:2], ident_f[:])
+                            if sorts(i) and tp == 0:
+                                words = s_tiles[i][:, col + u * P:col + (u + 1) * P]
+                            else:
+                                words = w32[:, col + u:col + 256:2]
+                            nc.tensor.transpose(bank[:, pos:pos + P], words, ident_f[:])
                     off = g * nt * 256 + tp * 512
                     dst = g32[:, off:off + 512].rearrange("p (c u) -> p c u", u=2)
                     srcv = bank[:].rearrange("p (u c) -> p c u", u=2)
-                    if i % V_PERIOD == 0 and 0 < i < V_LAST and tp == 1 and g == 1:
-                        nc.vector.tensor_copy(out=dst, in_=srcv)
-                    else:
-                        nc.scalar.copy(out=dst, in_=srcv)
+                    nc.scalar.copy(out=dst, in_=srcv)
                     if i < WARM_UNITS and 2 * tp + g in WARM_BANKS:
                         dummy()
                 if i == 0 and tp == 0:
@@ -295,6 +309,8 @@ def tile_dynamix_pb_kernel(tc, z, mlp_out, t2, A, W, h, out):
                 z_and_gate()
             if 0 <= s - LAG_M < nu:
                 multiply(s - LAG_M)
+            if sorts(s + 1):
+                sort_words(s + 1)
             if 0 <= s - LAG_S < nu:
                 mix(s - LAG_S)
                 if s - LAG_S in finish_after:

@@ -214,7 +214,7 @@ def tile_dynamix_pb_kernel(tc, z, mlp_out, t2, A, W, h, out):
             st = spool.tile([P, 1024], F32, name="st", tag="st")
             nc.vector.tensor_copy(
                 out=st[:].rearrange("p (x u k) -> p x u k", x=4, u=2),
-                in_=w_tiles[i][:, 0:2048].bitcast(F32).rearrange("p (x k u) -> p x u k", x=4, u=2),
+                in_=w_tiles[i][:, 2048:4096].bitcast(F32).rearrange("p (x k u) -> p x u k", x=4, u=2),
             )
             s_tiles[i] = st
 
@@ -230,8 +230,8 @@ def tile_dynamix_pb_kernel(tc, z, mlp_out, t2, A, W, h, out):
                         for t_ in range(2):
                             col = (2 * tp + t_) * 512 + 256 * g
                             pos = (2 * u + t_) * P
-                            if sorts(i) and tp == 0:
-                                words = s_tiles[i][:, col + u * P:col + (u + 1) * P]
+                            if sorts(i) and tp == 1:
+                                words = s_tiles[i][:, col - 1024 + u * P:col - 1024 + (u + 1) * P]
                             else:
                                 words = w32[:, col + u:col + 256:2]
                             nc.tensor.transpose(bank[:, pos:pos + P], words, ident_f[:])
@@ -309,12 +309,12 @@ def tile_dynamix_pb_kernel(tc, z, mlp_out, t2, A, W, h, out):
                 z_and_gate()
             if 0 <= s - LAG_M < nu:
                 multiply(s - LAG_M)
-            if sorts(s + 1):
-                sort_words(s + 1)
             if 0 <= s - LAG_S < nu:
                 mix(s - LAG_S)
                 if s - LAG_S in finish_after:
                     finish(finish_after[s - LAG_S][0], finish_after[s - LAG_S][1])
             if 1 <= s <= nu:
                 quantise(s - 1)
+            if sorts(s + 1):
+                sort_words(s + 1)
             side_vector(s)

@@ -22,8 +22,7 @@ FLOPS = 2 * E * M * M * B + 4 * E * M * B
 PIN = True
 W_BUFS = 12
 TP_BUFS = 5
-LAG_M = 3
-LAG_S = 4
+SHORT = 5
 PRE_WARM = 7
 WARM_UNITS = 3
 WARM_BANKS = (0, 1, 3)
@@ -47,7 +46,7 @@ def tile_dynamix_pb_kernel(tc, z, mlp_out, t2, A, W, h, out):
     with ExitStack() as ctx:
         const = ctx.enter_context(tc.tile_pool(name="const", bufs=1))
         wpool = ctx.enter_context(tc.tile_pool(name="wpool", bufs=W_BUFS))
-        gpool = ctx.enter_context(tc.tile_pool(name="gpool", bufs=3))
+        gpool = ctx.enter_context(tc.tile_pool(name="gpool", bufs=4))
         qpool = ctx.enter_context(tc.tile_pool(name="qpool", bufs=4))
         opool = ctx.enter_context(tc.tile_pool(name="opool", bufs=2))
         spool = ctx.enter_context(tc.tile_pool(name="spool", bufs=3))
@@ -80,24 +79,24 @@ def tile_dynamix_pb_kernel(tc, z, mlp_out, t2, A, W, h, out):
         warm2 = const.tile([P, 1], F32, name="warm2")
         nc.scalar.activation(out=warm2[:], in_=warm[:], func=ACT.Exp)
 
+        load_w(0, pieces=4)
         mlp = const.tile([P, E], BF16, name="mlp")
         nc.sync.dma_start(out=mlp[:], in_=mlp_out)
         t2b = const.tile([P, 1], BF16, name="t2b")
         nc.sync.dma_start(out=t2b[:], in_=t2.partition_broadcast(P))
-        load_w(0, pieces=2)
         zq = const.tile([P, 8 * B], BF16, name="zq")
         nc.sync.dma_start(
             out=zq[:].rearrange("p (c x) -> p c x", c=2),
             in_=z.rearrange("(c p e) b -> p c (e b)", c=2, p=P, e=4),
         )
-        for i in range(1, 4):
+        for i in range(1, 8):
             load_w(i)
         for s in range(3):
             nc.sync.dma_start(out=ah[16 * s:16 * s + 16, 0:M], in_=A)
             nc.sync.dma_start(out=ah[16 * s:16 * s + 16, M:2 * M], in_=h)
         zm = const.tile([P, 8 * B], BF16, name="zm")
         nc.sync.dma_start(out=zm[:], in_=z.rearrange("(p t) b -> p (t b)", t=8))
-        for i in range(4, W_BUFS):
+        for i in range(8, W_BUFS):
             load_w(i)
 
         dps = pm.tile([P, 512], F32, name="dps", tag="ps")
@@ -170,7 +169,7 @@ def tile_dynamix_pb_kernel(tc, z, mlp_out, t2, A, W, h, out):
         side = {}
 
         def side_tensor(s):
-            if s == 4:
+            if s == 8:
                 xp = pt.tile([P, P], BF16, name="xp", tag="tp")
                 nc.tensor.transpose(xp[:], xs[:], ident_b[:])
                 side["xp"] = xp
@@ -178,8 +177,8 @@ def tile_dynamix_pb_kernel(tc, z, mlp_out, t2, A, W, h, out):
                 for t in range(8):
                     nc.tensor.transpose(zp[:, t * P:(t + 1) * P], zm[:, t * P:(t + 1) * P], ident_b[:])
                 nc.scalar.copy(out=zt[:], in_=zp[:])
-            if 6 <= s <= 9:
-                hb, a = divmod(s - 6, 2)
+            if 10 <= s <= 13:
+                hb, a = divmod(s - 10, 2)
                 gb = pt.tile([P, 512], F32, name="gb", tag="tp")
                 col = (a * 8 + 4 * hb) * P
                 nc.tensor.matmul(gb[:], lhsT=rw[:], rhs=aht[:, col:col + 512], start=True, stop=True)
@@ -188,10 +187,10 @@ def tile_dynamix_pb_kernel(tc, z, mlp_out, t2, A, W, h, out):
         def side_vector(s):
             if s == 2:
                 gate_split()
-            if s == 4:
+            if s == 8:
                 nc.vector.tensor_copy(out=rw[:], in_=side["xp"][:])
-            if 6 <= s <= 9:
-                hb, a = divmod(s - 6, 2)
+            if 10 <= s <= 13:
+                hb, a = divmod(s - 10, 2)
                 sl = slice(hb * 512, (hb + 1) * 512)
                 if a == 0:
                     tmp = opool.tile([P, 512], F32, name="tmp", tag="tmp")
@@ -208,7 +207,7 @@ def tile_dynamix_pb_kernel(tc, z, mlp_out, t2, A, W, h, out):
         s_tiles = {}
 
         def sorts(i):
-            return FIRST_SORTED <= i < nu and units[i][2] == 4
+            return FIRST_SORTED <= i < nu - 3
 
         def sort_words(i):
             st = spool.tile([P, 1024], F32, name="st", tag="st")
@@ -297,8 +296,11 @@ def tile_dynamix_pb_kernel(tc, z, mlp_out, t2, A, W, h, out):
                 out=out.rearrange("(p t) b -> p (t b)", t=8)[:, t0 * P:(t0 + nt) * P], in_=fin[:, 0:nt * P]
             )
 
+        def at_step(s, lag):
+            return [i for i in range(nu) if i + lag - (i >= nu - SHORT) == s]
+
         next_load = W_BUFS
-        for s in range(nu + max(LAG_M, LAG_S)):
+        for s in range(nu + 4):
             if s < nu:
                 transposes(s)
                 if next_load < nu:
@@ -307,14 +309,14 @@ def tile_dynamix_pb_kernel(tc, z, mlp_out, t2, A, W, h, out):
             side_tensor(s)
             if s == 0:
                 z_and_gate()
-            if 0 <= s - LAG_M < nu:
-                multiply(s - LAG_M)
-            if 0 <= s - LAG_S < nu:
-                mix(s - LAG_S)
-                if s - LAG_S in finish_after:
-                    finish(finish_after[s - LAG_S][0], finish_after[s - LAG_S][1])
-            if 1 <= s <= nu:
-                quantise(s - 1)
+            for i in at_step(s, 3):
+                multiply(i)
             if sorts(s + 1):
                 sort_words(s + 1)
+            for i in at_step(s, 2):
+                quantise(i)
+            for i in at_step(s, 4):
+                mix(i)
+                if i in finish_after:
+                    finish(finish_after[i][0], finish_after[i][1])
             side_vector(s)

@@ -26,7 +26,6 @@ SHORT = 5
 PRE_WARM = 7
 WARM_UNITS = 3
 WARM_BANKS = (0, 1, 3)
-FIRST_SORTED = 2
 
 
 def make_units():
@@ -84,12 +83,15 @@ def tile_dynamix_pb_kernel(tc, z, mlp_out, t2, A, W, h, out):
         nc.sync.dma_start(out=mlp[:], in_=mlp_out)
         t2b = const.tile([P, 1], BF16, name="t2b")
         nc.sync.dma_start(out=t2b[:], in_=t2.partition_broadcast(P))
+        load_w(1)
         zq = const.tile([P, 8 * B], BF16, name="zq")
-        nc.sync.dma_start(
-            out=zq[:].rearrange("p (c x) -> p c x", c=2),
-            in_=z.rearrange("(c p e) b -> p c (e b)", c=2, p=P, e=4),
-        )
-        for i in range(1, 8):
+        nc.sync.dma_start(out=zq[:, 0:512], in_=z[0:512, :].rearrange("(p e) b -> p (e b)", e=4))
+        zhigh = z[512:1024, :].rearrange("(h u v e) b -> v h u (e b)", u=2, v=2, e=2)
+        for v in range(2):
+            nc.sync.dma_start(
+                out=zq[v:P:2, 512:1024].rearrange("p (u x) -> p u x", u=2), in_=zhigh[v]
+            )
+        for i in range(2, 8):
             load_w(i)
         for s in range(3):
             nc.sync.dma_start(out=ah[16 * s:16 * s + 16, 0:M], in_=A)
@@ -206,14 +208,13 @@ def tile_dynamix_pb_kernel(tc, z, mlp_out, t2, A, W, h, out):
 
         s_tiles = {}
 
-        def sorts(i):
-            return FIRST_SORTED <= i < nu - 3
-
         def sort_words(i):
+            nt = units[i][2]
             st = spool.tile([P, 1024], F32, name="st", tag="st")
+            w32 = w_tiles[i][:, 0:nt * M].bitcast(F32).rearrange("p (t g x) -> p t g x", t=nt, g=2)
             nc.vector.tensor_copy(
-                out=st[:].rearrange("p (x u k) -> p x u k", x=4, u=2),
-                in_=w_tiles[i][:, 2048:4096].bitcast(F32).rearrange("p (x k u) -> p x u k", x=4, u=2),
+                out=st[:, 0:nt * 256].rearrange("p (t u h v) -> p t u h v", t=nt, u=2, v=2),
+                in_=w32[:, :, 1, :].rearrange("p t (h u v) -> p t u h v", u=2, v=2),
             )
             s_tiles[i] = st
 
@@ -222,15 +223,16 @@ def tile_dynamix_pb_kernel(tc, z, mlp_out, t2, A, W, h, out):
             w32 = w_tiles[i][:].bitcast(F32)
             gt = gpool.tile([P, 4096], BF16, name="gt", tag="gt", align_bytes=64)
             g32 = gt[:].bitcast(F32)
-            for tp in range(nt // 2):
-                for g in range(2):
+            for g in range(2):
+                for tp in range(nt // 2):
                     bank = pt.tile([P, 512], F32, name="bank", tag="tp")
                     for u in range(2):
                         for t_ in range(2):
                             col = (2 * tp + t_) * 512 + 256 * g
                             pos = (2 * u + t_) * P
-                            if sorts(i) and tp == 1:
-                                words = s_tiles[i][:, col - 1024 + u * P:col - 1024 + (u + 1) * P]
+                            if g == 1:
+                                at = (2 * tp + t_) * 256 + u * P
+                                words = s_tiles[i][:, at:at + P]
                             else:
                                 words = w32[:, col + u:col + 256:2]
                             nc.tensor.transpose(bank[:, pos:pos + P], words, ident_f[:])
@@ -240,7 +242,7 @@ def tile_dynamix_pb_kernel(tc, z, mlp_out, t2, A, W, h, out):
                     nc.scalar.copy(out=dst, in_=srcv)
                     if i < WARM_UNITS and 2 * tp + g in WARM_BANKS:
                         dummy()
-                if i == 0 and tp == 0:
+                if i == 0 and g == 0:
                     gate_exp()
             g_tiles[i] = gt
 
@@ -299,24 +301,29 @@ def tile_dynamix_pb_kernel(tc, z, mlp_out, t2, A, W, h, out):
         def at_step(s, lag):
             return [i for i in range(nu) if i + lag - (i >= nu - SHORT) == s]
 
+        def at_step(s, lag):
+            return [i for i in range(nu) if i + lag - (i >= nu - SHORT) == s]
+
         next_load = W_BUFS
-        for s in range(nu + 4):
+        sort_words(0)
+        for s in range(nu + 5):
             if s < nu:
                 transposes(s)
                 if next_load < nu:
                     load_w(next_load)
                     next_load += 1
             side_tensor(s)
-            if s == 0:
+            if s == 1:
                 z_and_gate()
             for i in at_step(s, 3):
                 multiply(i)
-            if sorts(s + 1):
-                sort_words(s + 1)
+            for i in at_step(s - 1, 4):
+                if i in finish_after:
+                    finish(finish_after[i][0], finish_after[i][1])
             for i in at_step(s, 2):
                 quantise(i)
             for i in at_step(s, 4):
                 mix(i)
-                if i in finish_after:
-                    finish(finish_after[i][0], finish_after[i][1])
+            if s + 1 < nu:
+                sort_words(s + 1)
             side_vector(s)

@@ -59,11 +59,11 @@ def tile_dynamix_pb_kernel(tc, z, mlp_out, t2, A, W, h, out):
         def load_w(i, pieces=1):
             e, t0, nt = units[i]
             wt = wpool.tile([P, 4 * M], BF16, name="wt", tag="wt")
-            src = W[e].rearrange("(p t) k -> p (t k)", t=8)
+            src = W[e, 512 * (t0 // 4):512 * (t0 // 4) + 512, :].rearrange("(p t) k -> p (t k)", t=4)
             step = nt * M // pieces
             for c in range(pieces):
                 nc.sync.dma_start(
-                    out=wt[:, c * step:(c + 1) * step], in_=src[:, t0 * M + c * step:t0 * M + (c + 1) * step]
+                    out=wt[:, c * step:(c + 1) * step], in_=src[:, t0 % 4 * M + c * step:t0 % 4 * M + (c + 1) * step]
                 )
             w_tiles[i] = wt
 
@@ -97,7 +97,9 @@ def tile_dynamix_pb_kernel(tc, z, mlp_out, t2, A, W, h, out):
             nc.sync.dma_start(out=ah[16 * s:16 * s + 16, 0:M], in_=A)
             nc.sync.dma_start(out=ah[16 * s:16 * s + 16, M:2 * M], in_=h)
         zm = const.tile([P, 8 * B], BF16, name="zm")
-        nc.sync.dma_start(out=zm[:], in_=z.rearrange("(p t) b -> p (t b)", t=8))
+        nc.sync.dma_start(
+            out=zm[:].rearrange("p (h x) -> p h x", h=2), in_=z.rearrange("(h p t) b -> p h (t b)", h=2, t=4)
+        )
         for i in range(8, W_BUFS):
             load_w(i)
 
@@ -115,8 +117,8 @@ def tile_dynamix_pb_kernel(tc, z, mlp_out, t2, A, W, h, out):
         make_identity(nc, ident_b[:])
         aht = const.tile([P, 2 * M], BF16, name="aht")
         nc.gpsimd.tensor_scalar(
-            out=aht[:].rearrange("k (a t p) -> k a t p", a=2, t=8),
-            in0=ah[:].rearrange("k (a p t) -> k a t p", a=2, t=8),
+            out=aht[:].rearrange("k (a t p) -> k a t p", a=4, t=4),
+            in0=ah[:].rearrange("k (a p t) -> k a t p", a=4, t=4),
             scalar1=1.0, scalar2=0.0, op0=ALU.mult, op1=ALU.add,
         )
 
@@ -295,7 +297,10 @@ def tile_dynamix_pb_kernel(tc, z, mlp_out, t2, A, W, h, out):
             fin = opool.tile([P, 512], F32, name="fin", tag="fin")
             nc.scalar.copy(out=fin[:, 0:nt * P], in_=fb[:, 0:nt * P])
             nc.sync.dma_start(
-                out=out.rearrange("(p t) b -> p (t b)", t=8)[:, t0 * P:(t0 + nt) * P], in_=fin[:, 0:nt * P]
+                out=out[512 * (t0 // 4):512 * (t0 // 4) + 512, :].rearrange("(p t) b -> p (t b)", t=4)[
+                    :, t0 % 4 * P:(t0 % 4 + nt) * P
+                ],
+                in_=fin[:, 0:nt * P],
             )
 
         def at_step(s, lag):

@@ -116,11 +116,13 @@ def tile_dynamix_pb_kernel(tc, z, mlp_out, t2, A, W, h, out):
         ident_b = const.tile([P, P], BF16, name="ident_b")
         make_identity(nc, ident_b[:])
         aht = const.tile([P, 2 * M], BF16, name="aht")
-        nc.gpsimd.tensor_scalar(
-            out=aht[:].rearrange("k (a t p) -> k a t p", a=4, t=4),
-            in0=ah[:].rearrange("k (a p t) -> k a t p", a=4, t=4),
-            scalar1=1.0, scalar2=0.0, op0=ALU.mult, op1=ALU.add,
-        )
+
+        def order_ah():
+            nc.gpsimd.tensor_scalar(
+                out=aht[:].rearrange("k (a t p) -> k a t p", a=4, t=4),
+                in0=ah[:].rearrange("k (a p t) -> k a t p", a=4, t=4),
+                scalar1=1.0, scalar2=0.0, op0=ALU.mult, op1=ALU.add,
+            )
 
         mask = const.tile([P, 1], F32, name="mask")
         nc.vector.tensor_reduce(out=mask[:], in_=ident_f[:, 120:128], axis=AX.X, op=ALU.add)
@@ -181,8 +183,8 @@ def tile_dynamix_pb_kernel(tc, z, mlp_out, t2, A, W, h, out):
                 for t in range(8):
                     nc.tensor.transpose(zp[:, t * P:(t + 1) * P], zm[:, t * P:(t + 1) * P], ident_b[:])
                 nc.scalar.copy(out=zt[:], in_=zp[:])
-            if 10 <= s <= 13:
-                hb, a = divmod(s - 10, 2)
+            if 12 <= s <= 15:
+                hb, a = divmod(s - 12, 2)
                 gb = pt.tile([P, 512], F32, name="gb", tag="tp")
                 col = (a * 8 + 4 * hb) * P
                 nc.tensor.matmul(gb[:], lhsT=rw[:], rhs=aht[:, col:col + 512], start=True, stop=True)
@@ -193,8 +195,8 @@ def tile_dynamix_pb_kernel(tc, z, mlp_out, t2, A, W, h, out):
                 gate_split()
             if s == 8:
                 nc.vector.tensor_copy(out=rw[:], in_=side["xp"][:])
-            if 10 <= s <= 13:
-                hb, a = divmod(s - 10, 2)
+            if 12 <= s <= 15:
+                hb, a = divmod(s - 12, 2)
                 sl = slice(hb * 512, (hb + 1) * 512)
                 if a == 0:
                     tmp = opool.tile([P, 512], F32, name="tmp", tag="tmp")
@@ -212,9 +214,9 @@ def tile_dynamix_pb_kernel(tc, z, mlp_out, t2, A, W, h, out):
 
         def sort_words(i):
             nt = units[i][2]
-            st = spool.tile([P, 1024], F32, name="st", tag="st")
-            w32 = w_tiles[i][:, 0:nt * M].bitcast(F32).rearrange("p (t g x) -> p t g x", t=nt, g=2)
-            nc.vector.tensor_copy(
+            st = spool.tile([P, 1024], U32, name="st", tag="st")
+            w32 = w_tiles[i][:, 0:nt * M].bitcast(U32).rearrange("p (t g x) -> p t g x", t=nt, g=2)
+            nc.gpsimd.tensor_copy(
                 out=st[:, 0:nt * 256].rearrange("p (t u h v) -> p t u h v", t=nt, u=2, v=2),
                 in_=w32[:, :, 1, :].rearrange("p t (h u v) -> p t u h v", u=2, v=2),
             )
@@ -234,7 +236,7 @@ def tile_dynamix_pb_kernel(tc, z, mlp_out, t2, A, W, h, out):
                             pos = (2 * u + t_) * P
                             if g == 1:
                                 at = (2 * tp + t_) * 256 + u * P
-                                words = s_tiles[i][:, at:at + P]
+                                words = s_tiles[i][:, at:at + P].bitcast(F32)
                             else:
                                 words = w32[:, col + u:col + 256:2]
                             nc.tensor.transpose(bank[:, pos:pos + P], words, ident_f[:])
@@ -331,4 +333,6 @@ def tile_dynamix_pb_kernel(tc, z, mlp_out, t2, A, W, h, out):
                 mix(i)
             if s + 1 < nu:
                 sort_words(s + 1)
+            if s == 9:
+                order_ah()
             side_vector(s)

@@ -23,7 +23,7 @@ PIN = True
 W_BUFS = 12
 TP_BUFS = 5
 SHORT = 5
-PRE_WARM = 7
+PRE_WARM = 5
 WARM_UNITS = 3
 WARM_BANKS = (0, 1, 3)
 
@@ -47,7 +47,7 @@ def tile_dynamix_pb_kernel(tc, z, mlp_out, t2, A, W, h, out):
         wpool = ctx.enter_context(tc.tile_pool(name="wpool", bufs=W_BUFS))
         gpool = ctx.enter_context(tc.tile_pool(name="gpool", bufs=4))
         qpool = ctx.enter_context(tc.tile_pool(name="qpool", bufs=4))
-        opool = ctx.enter_context(tc.tile_pool(name="opool", bufs=2))
+        opool = ctx.enter_context(tc.tile_pool(name="opool", bufs=3))
         spool = ctx.enter_context(tc.tile_pool(name="spool", bufs=3))
         pt = ctx.enter_context(tc.psum_pool(name="pt", bufs=TP_BUFS))
         pm = ctx.enter_context(tc.psum_pool(name="pm", bufs=8 - TP_BUFS))
@@ -85,13 +85,10 @@ def tile_dynamix_pb_kernel(tc, z, mlp_out, t2, A, W, h, out):
         nc.sync.dma_start(out=t2b[:], in_=t2.partition_broadcast(P))
         load_w(1)
         zq = const.tile([P, 8 * B], BF16, name="zq")
-        nc.sync.dma_start(out=zq[:, 0:512], in_=z[0:512, :].rearrange("(p e) b -> p (e b)", e=4))
-        zhigh = z[512:1024, :].rearrange("(h u v e) b -> v h u (e b)", u=2, v=2, e=2)
-        for v in range(2):
-            nc.sync.dma_start(
-                out=zq[v:P:2, 512:1024].rearrange("p (u x) -> p u x", u=2), in_=zhigh[v]
-            )
-        for i in range(2, 8):
+        nc.sync.dma_start(
+            out=zq[:].rearrange("p (c x) -> p c x", c=2), in_=z.rearrange("(c p e) b -> p c (e b)", c=2, e=4)
+        )
+        for i in range(2, W_BUFS):
             load_w(i)
         for s in range(3):
             nc.sync.dma_start(out=ah[16 * s:16 * s + 16, 0:M], in_=A)
@@ -100,8 +97,6 @@ def tile_dynamix_pb_kernel(tc, z, mlp_out, t2, A, W, h, out):
         nc.sync.dma_start(
             out=zm[:].rearrange("p (h x) -> p h x", h=2), in_=z.rearrange("(h p t) b -> p h (t b)", h=2, t=4)
         )
-        for i in range(8, W_BUFS):
-            load_w(i)
 
         dps = pm.tile([P, 512], F32, name="dps", tag="ps")
 
@@ -175,7 +170,7 @@ def tile_dynamix_pb_kernel(tc, z, mlp_out, t2, A, W, h, out):
         side = {}
 
         def side_tensor(s):
-            if s == 8:
+            if s == 12:
                 xp = pt.tile([P, P], BF16, name="xp", tag="tp")
                 nc.tensor.transpose(xp[:], xs[:], ident_b[:])
                 side["xp"] = xp
@@ -183,8 +178,8 @@ def tile_dynamix_pb_kernel(tc, z, mlp_out, t2, A, W, h, out):
                 for t in range(8):
                     nc.tensor.transpose(zp[:, t * P:(t + 1) * P], zm[:, t * P:(t + 1) * P], ident_b[:])
                 nc.scalar.copy(out=zt[:], in_=zp[:])
-            if 12 <= s <= 15:
-                hb, a = divmod(s - 12, 2)
+            if 16 <= s <= 19:
+                hb, a = divmod(s - 16, 2)
                 gb = pt.tile([P, 512], F32, name="gb", tag="tp")
                 col = (a * 8 + 4 * hb) * P
                 nc.tensor.matmul(gb[:], lhsT=rw[:], rhs=aht[:, col:col + 512], start=True, stop=True)
@@ -193,10 +188,10 @@ def tile_dynamix_pb_kernel(tc, z, mlp_out, t2, A, W, h, out):
         def side_vector(s):
             if s == 2:
                 gate_split()
-            if s == 8:
+            if s == 12:
                 nc.vector.tensor_copy(out=rw[:], in_=side["xp"][:])
-            if 12 <= s <= 15:
-                hb, a = divmod(s - 12, 2)
+            if 16 <= s <= 19:
+                hb, a = divmod(s - 16, 2)
                 sl = slice(hb * 512, (hb + 1) * 512)
                 if a == 0:
                     tmp = opool.tile([P, 512], F32, name="tmp", tag="tmp")
@@ -211,14 +206,16 @@ def tile_dynamix_pb_kernel(tc, z, mlp_out, t2, A, W, h, out):
         m_tiles = {}
 
         s_tiles = {}
+        vector_copies = []
+
+        def sorts(i):
+            return 0 < i < nu and units[i][2] == 4
 
         def sort_words(i):
-            nt = units[i][2]
-            st = spool.tile([P, 1024], U32, name="st", tag="st")
-            w32 = w_tiles[i][:, 0:nt * M].bitcast(U32).rearrange("p (t g x) -> p t g x", t=nt, g=2)
+            st = spool.tile([P, 768], U32, name="st", tag="st")
             nc.gpsimd.tensor_copy(
-                out=st[:, 0:nt * 256].rearrange("p (t u h v) -> p t u h v", t=nt, u=2, v=2),
-                in_=w32[:, :, 1, :].rearrange("p t (h u v) -> p t u h v", u=2, v=2),
+                out=st[:].rearrange("p (x u k) -> p x u k", x=3, u=2),
+                in_=w_tiles[i][:, 2560:4096].bitcast(U32).rearrange("p (x k u) -> p x u k", x=3, u=2),
             )
             s_tiles[i] = st
 
@@ -227,15 +224,15 @@ def tile_dynamix_pb_kernel(tc, z, mlp_out, t2, A, W, h, out):
             w32 = w_tiles[i][:].bitcast(F32)
             gt = gpool.tile([P, 4096], BF16, name="gt", tag="gt", align_bytes=64)
             g32 = gt[:].bitcast(F32)
-            for g in range(2):
-                for tp in range(nt // 2):
+            for tp in range(nt // 2):
+                for g in range(2):
                     bank = pt.tile([P, 512], F32, name="bank", tag="tp")
                     for u in range(2):
                         for t_ in range(2):
                             col = (2 * tp + t_) * 512 + 256 * g
                             pos = (2 * u + t_) * P
-                            if g == 1:
-                                at = (2 * tp + t_) * 256 + u * P
+                            at = col - 1280 + u * P
+                            if sorts(i) and at >= 0:
                                 words = s_tiles[i][:, at:at + P].bitcast(F32)
                             else:
                                 words = w32[:, col + u:col + 256:2]
@@ -243,10 +240,13 @@ def tile_dynamix_pb_kernel(tc, z, mlp_out, t2, A, W, h, out):
                     off = g * nt * 256 + tp * 512
                     dst = g32[:, off:off + 512].rearrange("p (c u) -> p c u", u=2)
                     srcv = bank[:].rearrange("p (u c) -> p c u", u=2)
-                    nc.scalar.copy(out=dst, in_=srcv)
+                    if i % 3 > 0 and i < nu - SHORT and tp == 0 and g == 1:
+                        vector_copies.append((dst, srcv))
+                    else:
+                        nc.scalar.copy(out=dst, in_=srcv)
                     if i < WARM_UNITS and 2 * tp + g in WARM_BANKS:
                         dummy()
-                if i == 0 and g == 0:
+                if i == 0 and tp == 0:
                     gate_exp()
             g_tiles[i] = gt
 
@@ -312,7 +312,6 @@ def tile_dynamix_pb_kernel(tc, z, mlp_out, t2, A, W, h, out):
             return [i for i in range(nu) if i + lag - (i >= nu - SHORT) == s]
 
         next_load = W_BUFS
-        sort_words(0)
         for s in range(nu + 5):
             if s < nu:
                 transposes(s)
@@ -329,10 +328,13 @@ def tile_dynamix_pb_kernel(tc, z, mlp_out, t2, A, W, h, out):
                     finish(finish_after[i][0], finish_after[i][1])
             for i in at_step(s, 2):
                 quantise(i)
+            for dst, srcv in vector_copies:
+                nc.vector.tensor_copy(out=dst, in_=srcv)
+            vector_copies.clear()
             for i in at_step(s, 4):
                 mix(i)
-            if s + 1 < nu:
+            if sorts(s + 1):
                 sort_words(s + 1)
-            if s == 9:
+            if s == 13:
                 order_ah()
             side_vector(s)

from contextlib import ExitStack

import concourse.mybir as mybir
from concourse.masks import make_identity

F32 = mybir.dt.float32
BF16 = mybir.dt.bfloat16
I32 = mybir.dt.int32
U32 = mybir.dt.uint32
U8 = mybir.dt.uint8
FP8X4 = mybir.dt.float8_e4m3fn_x4
ALU = mybir.AluOpType
ACT = mybir.ActivationFunctionType
AX = mybir.AxisListType

P = 128
M = 1024
E = 16
B = 128
FLOPS = 2 * E * M * M * B + 4 * E * M * B

PIN = True
W_BUFS = 12
TP_BUFS = 5
SHORT = 5
PRE_WARM = 5
WARM_UNITS = 3
WARM_BANKS = (0, 1, 3)


def make_units():
    units = []
    for e in range(E - 2):
        units.append((e, 0, 4))
        units.append((e, 4, 4))
    units.extend([(E - 2, 0, 4), (E - 1, 0, 4), (E - 2, 4, 4), (E - 1, 4, 2), (E - 1, 6, 2)])
    return units


def tile_dynamix_pb_kernel(tc, z, mlp_out, t2, A, W, h, out):
    nc = tc.nc
    units = make_units()
    nu = len(units)
    finish_after = {29: (0, 4), 31: (4, 2), 32: (6, 2)}
    with ExitStack() as ctx:
        const = ctx.enter_context(tc.tile_pool(name="const", bufs=1))
        wpool = ctx.enter_context(tc.tile_pool(name="wpool", bufs=W_BUFS))
        gpool = ctx.enter_context(tc.tile_pool(name="gpool", bufs=4))
        qpool = ctx.enter_context(tc.tile_pool(name="qpool", bufs=4))
        opool = ctx.enter_context(tc.tile_pool(name="opool", bufs=3))
        spool = ctx.enter_context(tc.tile_pool(name="spool", bufs=3))
        pt = ctx.enter_context(tc.psum_pool(name="pt", bufs=TP_BUFS))
        pm = ctx.enter_context(tc.psum_pool(name="pm", bufs=8 - TP_BUFS))
        if PIN:
            ctx.enter_context(tc.manual_schedule())

        w_tiles = {}

        def load_w(i, pieces=1):
            e, t0, nt = units[i]
            wt = wpool.tile([P, 4 * M], BF16, name="wt", tag="wt")
            src = W[e, 512 * (t0 // 4):512 * (t0 // 4) + 512, :].rearrange("(p t) k -> p (t k)", t=4)
            step = nt * M // pieces
            for c in range(pieces):
                nc.sync.dma_start(
                    out=wt[:, c * step:(c + 1) * step], in_=src[:, t0 % 4 * M + c * step:t0 % 4 * M + (c + 1) * step]
                )
            w_tiles[i] = wt

        warm = const.tile([P, 1], F32, name="warm")
        nc.vector.memset(warm[:], 0.0)
        dz = const.tile([P, 512], BF16, name="dz")
        nc.vector.memset(dz[:].bitcast(I32), 0)
        ah = const.tile([P, 2 * M], BF16, name="ah")
        nc.vector.memset(ah[:].bitcast(I32), 0)
        xs = const.tile([P, P], BF16, name="xs")
        nc.vector.memset(xs[:].bitcast(I32), 0)
        warm2 = const.tile([P, 1], F32, name="warm2")
        nc.scalar.activation(out=warm2[:], in_=warm[:], func=ACT.Exp)

        load_w(0, pieces=4)
        mlp = const.tile([P, E], BF16, name="mlp")
        nc.sync.dma_start(out=mlp[:], in_=mlp_out)
        t2b = const.tile([P, 1], BF16, name="t2b")
        nc.sync.dma_start(out=t2b[:], in_=t2.partition_broadcast(P))
        load_w(1)
        zq = const.tile([P, 8 * B], BF16, name="zq")
        nc.sync.dma_start(
            out=zq[:].rearrange("p (c x) -> p c x", c=2), in_=z.rearrange("(c p e) b -> p c (e b)", c=2, e=4)
        )
        for i in range(2, W_BUFS):
            load_w(i)
        for s in range(3):
            nc.sync.dma_start(out=ah[16 * s:16 * s + 16, 0:M], in_=A)
            nc.sync.dma_start(out=ah[16 * s:16 * s + 16, M:2 * M], in_=h)
        zm = const.tile([P, 8 * B], BF16, name="zm")
        nc.sync.dma_start(
            out=zm[:].rearrange("p (h x) -> p h x", h=2), in_=z.rearrange("(h p t) b -> p h (t b)", h=2, t=4)
        )

        dps = pm.tile([P, 512], F32, name="dps", tag="ps")

        def dummy():
            nc.tensor.matmul(dps[:], lhsT=dz[:, 0:P], rhs=dz[:], start=True, stop=True)

        for c in range(PRE_WARM):
            dummy()

        ident_f = const.tile([P, P], F32, name="ident_f")
        make_identity(nc, ident_f[:])
        ident_b = const.tile([P, P], BF16, name="ident_b")
        make_identity(nc, ident_b[:])
        aht = const.tile([P, 2 * M], BF16, name="aht")

        def order_ah():
            nc.gpsimd.tensor_scalar(
                out=aht[:].rearrange("k (a t p) -> k a t p", a=4, t=4),
                in0=ah[:].rearrange("k (a p t) -> k a t p", a=4, t=4),
                scalar1=1.0, scalar2=0.0, op0=ALU.mult, op1=ALU.add,
            )

        mask = const.tile([P, 1], F32, name="mask")
        nc.vector.tensor_reduce(out=mask[:], in_=ident_f[:, 120:128], axis=AX.X, op=ALU.add)
        floor = const.tile([P, 1], F32, name="floor")
        nc.vector.tensor_scalar(out=floor[:], in0=mask[:], scalar1=-1.0, scalar2=3.4e38, op0=ALU.add, op1=ALU.mult)

        rt = const.tile([P, 1], F32, name="rt")
        nc.vector.reciprocal(out=rt[:], in_=t2b[:])
        lg = const.tile([P, E], F32, name="lg")
        nc.vector.tensor_scalar(out=lg[:], in0=mlp[:], scalar1=rt[:, 0:1], scalar2=-1.0, op0=ALU.mult, op1=ALU.mult)
        mx = const.tile([P, 1], F32, name="mx")
        nc.vector.tensor_reduce(out=mx[:], in_=lg[:], axis=AX.X, op=ALU.max)
        nmx = const.tile([P, 1], F32, name="nmx")
        nc.vector.tensor_scalar(out=nmx[:], in0=mx[:], scalar1=-1.0, scalar2=None, op0=ALU.mult)
        ex = const.tile([P, E], F32, name="ex")
        sm = const.tile([P, 1], F32, name="sm")
        rs = const.tile([P, 1], F32, name="rs")
        wg = const.tile([P, E], F32, name="wg")
        zg = const.tile([P, 8 * B], BF16, name="zg", align_bytes=64)
        zc = const.tile([P, 2 * B], U32, name="zc", align_bytes=64)
        zs = const.tile([P, 2 * B], U8, name="zs", align_bytes=64)
        acc = const.tile([P, M], F32, name="acc")
        rw = const.tile([P, B], BF16, name="rw")
        zt = const.tile([P, M], BF16, name="zt")

        def gate_exp():
            nc.scalar.activation(out=ex[:], in_=lg[:], func=ACT.Exp, bias=nmx[:, 0:1], scale=1.0, accum_out=sm[:])

        def z_and_gate():
            nc.vector.tensor_scalar(
                out=zq[:, 512:1024], in0=zq[:, 512:1024], scalar1=floor[:, 0:1], scalar2=None, op0=ALU.max
            )
            nc.vector.tensor_copy(
                out=zg[:].rearrange("p (g b j) -> p g b j", g=2, j=4),
                in_=zq[:].rearrange("p (g j b) -> p g b j", g=2, j=4),
            )
            nc.vector.reciprocal(out=rs[:], in_=sm[:])
            nc.vector.tensor_scalar(out=wg[:], in0=ex[:], scalar1=rs[:, 0:1], scalar2=None, op0=ALU.mult)
            nc.vector.quantize_mx(out=zc[:].bitcast(FP8X4), scales=zs[:], in_=zg[:])

        def gate_split():
            nc.vector.tensor_copy(out=xs[:, 0:16], in_=wg[:])
            r1 = const.tile([P, E], F32, name="r1")
            nc.vector.tensor_tensor(out=r1[:], in0=wg[:], in1=xs[:, 0:16], op=ALU.subtract)
            nc.vector.tensor_copy(out=xs[:, 16:32], in_=r1[:])
            r2 = const.tile([P, E], F32, name="r2")
            nc.vector.tensor_tensor(out=r2[:], in0=r1[:], in1=xs[:, 16:32], op=ALU.subtract)
            nc.vector.tensor_copy(out=xs[:, 32:48], in_=r2[:])

        side = {}

        def side_tensor(s):
            if s == 12:
                xp = pt.tile([P, P], BF16, name="xp", tag="tp")
                nc.tensor.transpose(xp[:], xs[:], ident_b[:])
                side["xp"] = xp
                zp = pt.tile([P, M], BF16, name="zp", tag="tp")
                for t in range(8):
                    nc.tensor.transpose(zp[:, t * P:(t + 1) * P], zm[:, t * P:(t + 1) * P], ident_b[:])
                nc.scalar.copy(out=zt[:], in_=zp[:])
            if 16 <= s <= 19:
                hb, a = divmod(s - 16, 2)
                gb = pt.tile([P, 512], F32, name="gb", tag="tp")
                col = (a * 8 + 4 * hb) * P
                nc.tensor.matmul(gb[:], lhsT=rw[:], rhs=aht[:, col:col + 512], start=True, stop=True)
                side["gb"] = gb

        def side_vector(s):
            if s == 2:
                gate_split()
            if s == 12:
                nc.vector.tensor_copy(out=rw[:], in_=side["xp"][:])
            if 16 <= s <= 19:
                hb, a = divmod(s - 16, 2)
                sl = slice(hb * 512, (hb + 1) * 512)
                if a == 0:
                    tmp = opool.tile([P, 512], F32, name="tmp", tag="tmp")
                    nc.vector.tensor_tensor(out=tmp[:], in0=side["gb"][:], in1=zt[:, sl], op=ALU.mult)
                    side["tmp"] = tmp
                else:
                    nc.vector.tensor_tensor(out=side["tmp"][:], in0=side["gb"][:], in1=side["tmp"][:], op=ALU.add)
                    nc.vector.tensor_tensor(out=acc[:, sl], in0=acc[:, sl], in1=side["tmp"][:], op=ALU.add)

        g_tiles = {}
        q_tiles = {}
        m_tiles = {}

        s_tiles = {}
        vector_copies = []

        def sorts(i):
            return 0 < i < nu and units[i][2] == 4

        def sort_words(i):
            st = spool.tile([P, 768], U32, name="st", tag="st")
            nc.gpsimd.tensor_copy(
                out=st[:].rearrange("p (x u k) -> p x u k", x=3, u=2),
                in_=w_tiles[i][:, 2560:4096].bitcast(U32).rearrange("p (x k u) -> p x u k", x=3, u=2),
            )
            s_tiles[i] = st

        def transposes(i):
            e, t0, nt = units[i]
            w32 = w_tiles[i][:].bitcast(F32)
            gt = gpool.tile([P, 4096], BF16, name="gt", tag="gt", align_bytes=64)
            g32 = gt[:].bitcast(F32)
            for tp in range(nt // 2):
                for g in range(2):
                    bank = pt.tile([P, 512], F32, name="bank", tag="tp")
                    for u in range(2):
                        for t_ in range(2):
                            col = (2 * tp + t_) * 512 + 256 * g
                            pos = (2 * u + t_) * P
                            at = col - 1280 + u * P
                            if sorts(i) and at >= 0:
                                words = s_tiles[i][:, at:at + P].bitcast(F32)
                            else:
                                words = w32[:, col + u:col + 256:2]
                            nc.tensor.transpose(bank[:, pos:pos + P], words, ident_f[:])
                    off = g * nt * 256 + tp * 512
                    dst = g32[:, off:off + 512].rearrange("p (c u) -> p c u", u=2)
                    srcv = bank[:].rearrange("p (u c) -> p c u", u=2)
                    if i % 3 > 0 and i < nu - SHORT and tp == 0 and g == 1:
                        vector_copies.append((dst, srcv))
                    else:
                        nc.scalar.copy(out=dst, in_=srcv)
                    if i < WARM_UNITS and 2 * tp + g in WARM_BANKS:
                        dummy()
                if i == 0 and tp == 0:
                    gate_exp()
            g_tiles[i] = gt

        def quantise(i):
            nt = units[i][2]
            cw = qpool.tile([P, 1024], U32, name="cw", tag="cw", align_bytes=64)
            cs = qpool.tile([P, 1024], U8, name="cs", tag="cs", align_bytes=64)
            nc.vector.quantize_mx(
                out=cw[:, 0:nt * 256].bitcast(FP8X4), scales=cs[:, 0:nt * 256], in_=g_tiles[i][:, 0:nt * 1024]
            )
            q_tiles[i] = (cw, cs)

        def multiply(i):
            e, t0, nt = units[i]
            cw, cs = q_tiles[i]
            n = nt * P
            ps = pm.tile([P, 512], F32, name="ps", tag="ps")
            c0 = 0
            for g in range(2):
                nc.tensor.matmul_mx(
                    out=ps[:, c0:c0 + n],
                    lhsT=zc[:, g * B:(g + 1) * B].bitcast(FP8X4),
                    lhsT_scale=zs[:, g * B:(g + 1) * B],
                    rhs=cw[:, g * n:(g + 1) * n].bitcast(FP8X4),
                    rhs_scale=cs[:, g * n:(g + 1) * n],
                    start=(g == 0),
                    stop=(g == 1),
                )
            m_tiles[i] = (ps, c0)

        def mix(i):
            e, t0, nt = units[i]
            ps, c0 = m_tiles[i]
            sl = slice(t0 * P, (t0 + nt) * P)
            if e == 0:
                nc.vector.tensor_scalar(
                    out=acc[:, sl], in0=ps[:, c0:c0 + nt * P], scalar1=wg[:, 0:1], scalar2=None, op0=ALU.mult
                )
            else:
                nc.vector.scalar_tensor_tensor(
                    out=acc[:, sl], in0=ps[:, c0:c0 + nt * P], scalar=wg[:, e:e + 1], in1=acc[:, sl],
                    op0=ALU.mult, op1=ALU.add,
                )

        def finish(t0, nt):
            fb = pt.tile([P, 512], F32, name="fb", tag="tp")
            for tl in range(nt):
                col = (t0 + tl) * P
                nc.tensor.transpose(fb[:, tl * P:(tl + 1) * P], acc[:, col:col + P], ident_f[:])
            fin = opool.tile([P, 512], F32, name="fin", tag="fin")
            nc.scalar.copy(out=fin[:, 0:nt * P], in_=fb[:, 0:nt * P])
            nc.sync.dma_start(
                out=out[512 * (t0 // 4):512 * (t0 // 4) + 512, :].rearrange("(p t) b -> p (t b)", t=4)[
                    :, t0 % 4 * P:(t0 % 4 + nt) * P
                ],
                in_=fin[:, 0:nt * P],
            )

        def at_step(s, lag):
            return [i for i in range(nu) if i + lag - (i >= nu - SHORT) == s]

        def at_step(s, lag):
            return [i for i in range(nu) if i + lag - (i >= nu - SHORT) == s]

        next_load = W_BUFS
        for s in range(nu + 5):
            if s < nu:
                transposes(s)
                if next_load < nu:
                    load_w(next_load)
                    next_load += 1
            side_tensor(s)
            if s == 1:
                z_and_gate()
            for i in at_step(s, 3):
                multiply(i)
            for i in at_step(s - 1, 4):
                if i in finish_after:
                    finish(finish_after[i][0], finish_after[i][1])
            for i in at_step(s, 2):
                quantise(i)
            for dst, srcv in vector_copies:
                nc.vector.tensor_copy(out=dst, in_=srcv)
            vector_copies.clear()
            for i in at_step(s, 4):
                mix(i)
            if sorts(s + 1):
                sort_words(s + 1)
            if s == 13:
                order_ah()
            side_vector(s)
